import numpy as np
import ml_dtypes


def mxq(x, axis, fmt="e4m3"):
    dtype, down = {"e4m3": (ml_dtypes.float8_e4m3fn, 7), "e5m2": (ml_dtypes.float8_e5m2, 14)}[fmt]
    v = np.moveaxis(np.asarray(x, np.float32).astype(ml_dtypes.bfloat16).astype(np.float64), axis, -1)
    blocks = v.reshape(v.shape[:-1] + (-1, 32))
    amax = np.abs(blocks).max(-1, keepdims=True)
    byte = np.maximum(np.where(amax > 0, np.frexp(amax)[1] - 1 + 127, 0) - down, 1)
    scale = np.exp2(byte - 127.0)
    codes = (blocks / scale).astype(np.float32).astype(dtype).astype(np.float64)
    return np.moveaxis((codes * scale).reshape(v.shape), -1, axis)


WIDE = False


def mx_kscale(k):
    if not WIDE:
        return np.ones(k)
    levels = np.array([30, -30])
    if k % 512:
        return np.exp2(np.random.permutation(np.resize(levels, k // 32))).repeat(32)
    a = np.empty((k // 512, 16))
    for p in range(k // 512):
        a[p, :8] = np.random.permutation(np.resize(levels, 8))
        for g in range(8):
            far = levels[np.abs(levels - a[p, g]) >= 10]
            a[p, g + 8] = far[np.random.randint(len(far))]
    return np.exp2(a.ravel()).repeat(32)


BF16 = ml_dtypes.bfloat16


def bf(x):
    return np.asarray(x, np.float32).astype(BF16)


def f64(x):
    return np.asarray(x).astype(np.float64)


B, S, H, NH, DH, G = 1, 512, 2048, 16, 128, 4
NKV = NH // G
ROPE_THETA = 10000.0


def rope(x):
    inv_freq = 1.0 / ROPE_THETA ** (np.arange(0, DH, 2) / DH)
    angles = np.arange(S)[:, None] * inv_freq[None, :]
    cos = np.cos(angles)[None, :, None, :]
    sin = np.sin(angles)[None, :, None, :]
    x1, x2 = np.split(x, 2, axis=-1)
    return np.concatenate([x1 * cos - x2 * sin, x1 * sin + x2 * cos], axis=-1)


def setup_inputs():
    s = mx_kscale(H)
    return {
        "hidden_states": bf(np.random.standard_normal((B, S, H)) * s),
        "Wq": bf(np.random.standard_normal((H, NH * DH)) * 1.4 / np.sqrt(H) / s[:, None]),
        "bq": bf(np.random.standard_normal(NH * DH) * 0.2),
        "Wk": bf(np.random.standard_normal((H, NKV * DH)) * 1.4 / np.sqrt(H) / s[:, None]),
        "bk": bf(np.random.standard_normal(NKV * DH) * 0.2),
        "Wv": bf(np.random.standard_normal((H, NKV * DH)) / np.sqrt(H) / s[:, None]),
        "bv": bf(np.random.standard_normal(NKV * DH) * 0.2),
    }


def reference(hidden_states, Wq, bq, Wk, bk, Wv, bv):
    xq = mxq(f64(hidden_states), 2, "e5m2")
    q = ((xq @ mxq(f64(Wq), 0, "e4m3")) + f64(bq)).reshape(B, S, NH, DH)
    k = ((xq @ mxq(f64(Wk), 0, "e4m3")) + f64(bk)).reshape(B, S, NKV, DH)
    v = ((xq @ mxq(f64(Wv), 0, "e4m3")) + f64(bv)).reshape(B, S, NKV, DH)
    q = rope(q)
    k = rope(k)
    return q.transpose(0, 2, 1, 3), k.transpose(0, 2, 1, 3), v.transpose(0, 2, 1, 3)

@@ -1,0 +1,302 @@
+import math
+from contextlib import ExitStack
+
+import concourse.mybir as mybir
+from concourse.masks import make_identity
+
+S, H, NH, NKV, DH = 512, 2048, 16, 4, 128
+ROPE_THETA = 10000.0
+FLOPS = 2 * S * H * (NH + 2 * NKV) * DH
+
+F32 = mybir.dt.float32
+BF16 = mybir.dt.bfloat16
+I32 = mybir.dt.int32
+U32 = mybir.dt.uint32
+U8 = mybir.dt.uint8
+E4M3X4 = mybir.dt.float8_e4m3fn_x4
+E5M2X4 = mybir.dt.float8_e5m2_x4
+ALU = mybir.AluOpType
+ACT = mybir.ActivationFunctionType
+
+P = 128
+PACK = 4
+K_PASS = P * PACK
+PASSES = H // K_PASS
+TOK_PER_P = S // P
+CHUNK = 512
+PAIR = 2 * DH
+RUN = 4
+VECTOR_COLS = 288
+
+
+def tile_autoreggqaattention_pa_kernel(
+    tc, hidden_states, Wq, bq, Wk, bk, Wv, bv, out_0, out_1, out_2
+):
+    nc = tc.nc
+    pairs = []
+    for w, out, heads, bias0, rotated in (
+        (Wk, out_1, NKV, NH, True),
+        (Wq, out_0, NH, 0, True),
+        (Wv, out_2, NKV, NH + NKV, False),
+    ):
+        for h in range(0, heads, 2):
+            pairs.append((w, h * DH, out, h, bias0 + h, rotated))
+    n_pairs = len(pairs)
+
+    with ExitStack() as ctx:
+        const = ctx.enter_context(tc.tile_pool(name="const", bufs=1))
+        loads = ctx.enter_context(tc.tile_pool(name="loads", bufs=16))
+        work = ctx.enter_context(tc.tile_pool(name="work", bufs=3))
+        results = ctx.enter_context(tc.tile_pool(name="results", bufs=20))
+        psum = ctx.enter_context(tc.psum_pool(name="psum", bufs=4))
+        ctx.enter_context(tc.manual_schedule())
+
+        x_rows = hidden_states[0].rearrange("(p j) k -> p j k", j=TOK_PER_P)
+        x_raw = []
+        for g in range(PASSES):
+            raw = loads.tile([P, TOK_PER_P, K_PASS], BF16, tag="raw", name="x_raw")
+            nc.sync.dma_start(out=raw[:], in_=x_rows[:, :, g * K_PASS : (g + 1) * K_PASS])
+            x_raw.append(raw)
+        w_raw = {}
+        for n in range(0, n_pairs, 2):
+            w, col0 = pairs[n][0], pairs[n][1]
+            for g in range(PASSES):
+                raw = loads.tile([P, PACK, CHUNK], BF16, tag="raw", name="w_raw")
+                rows = w[g * K_PASS : (g + 1) * K_PASS, col0 : col0 + CHUNK]
+                nc.sync.dma_start(out=raw[:], in_=rows.rearrange("(p t) c -> p t c", t=PACK))
+                w_raw[(n // 2, g)] = raw
+
+        channel = const.tile([P, 7], I32)
+        nc.gpsimd.iota(channel[:], pattern=[[0, 7]], base=0, channel_multiplier=1)
+        shifts = const.tile([P, 7], I32)
+        nc.gpsimd.iota(shifts[:], pattern=[[1, 7]], base=0, channel_multiplier=0)
+        position = const.tile([P, S], F32)
+        nc.gpsimd.iota(
+            position[:], pattern=[[1, TOK_PER_P], [TOK_PER_P, P]], base=0, channel_multiplier=0,
+            allow_small_or_imprecise_dtypes=True,
+        )
+        eye = const.tile([P, P + DH // 2], F32)
+        make_identity(nc, eye[:, 0:P])
+        nc.gpsimd.tensor_copy(out=eye[:, P : P + DH // 2], in_=eye[:, 0 : DH // 2])
+        identity = eye[:, 0:P]
+        swap_halves = eye[:, DH // 2 : DH // 2 + P]
+
+        bias_rows = const.tile([P, DH], BF16)
+        nc.vector.memset(bias_rows[:], 0.0)
+        nc.scalar.dma_start(out=bias_rows[0:NH, :], in_=bq.rearrange("(h d) -> h d", d=DH))
+        nc.scalar.dma_start(out=bias_rows[NH : NH + NKV, :], in_=bk.rearrange("(h d) -> h d", d=DH))
+        nc.scalar.dma_start(
+            out=bias_rows[NH + NKV : NH + 2 * NKV, :], in_=bv.rearrange("(h d) -> h d", d=DH)
+        )
+
+        shifted = const.tile([P, 7], I32)
+        nc.vector.tensor_tensor(out=shifted[:], in0=channel[:], in1=shifts[:], op=ALU.logical_shift_right)
+        bits = const.tile([P, 7], I32)
+        nc.vector.tensor_scalar(out=bits[:], in0=shifted[:], scalar1=1, scalar2=None, op0=ALU.bitwise_and)
+        factors = const.tile([P, 7], F32)
+        turn = 1.0 / (2.0 * math.pi)
+        for b in range(7):
+            off, on = (1.0, ROPE_THETA ** (-(2**b) / 64)) if b < 6 else (turn, -turn)
+            nc.vector.tensor_scalar(
+                out=factors[:, b : b + 1], in0=bits[:, b : b + 1], scalar1=on - off, scalar2=off,
+                op0=ALU.mult, op1=ALU.add,
+            )
+        freq = const.tile([P, 1], F32)
+        nc.vector.tensor_reduce(out=freq[:], in_=factors[:], axis=mybir.AxisListType.X, op=ALU.mult)
+        whole = const.tile([P, 2, S], I32)
+        frac = const.tile([P, 2, S], F32)
+        table = const.tile([P, 2, S], F32)
+        shift_turns = (0.25, 0.0)
+        for i in range(2):
+            nc.vector.tensor_scalar(
+                out=whole[:, i, :], in0=position[:], scalar1=freq[:], scalar2=shift_turns[i],
+                op0=ALU.mult, op1=ALU.add,
+            )
+        for i in range(2):
+            nc.vector.scalar_tensor_tensor(
+                out=frac[:, i, :], in0=position[:], scalar=freq[:], in1=whole[:, i, :],
+                op0=ALU.mult, op1=ALU.subtract,
+            )
+            nc.scalar.activation(
+                out=table[:, i, :], in_=frac[:, i, :], func=ACT.Sin,
+                scale=2.0 * math.pi, bias=2.0 * math.pi * shift_turns[i],
+            )
+        bias_rows32 = const.tile([P, DH], F32)
+        nc.vector.tensor_copy(out=bias_rows32[:], in_=bias_rows[:])
+
+        x_codes = const.tile([P, PASSES, S], U32, align_bytes=64)
+        x_scales = const.tile([P, PASSES, S], U8, align_bytes=64)
+        x_grouped = {}
+
+        def transpose_x(g):
+            grouped = work.tile([P, S * PACK], BF16, tag="x_grouped", name="x_grouped", align_bytes=64)
+            words = x_raw[g][:].bitcast(F32)
+            grouped_words = grouped[:].bitcast(F32).rearrange("p (j r u) -> p j r u", j=TOK_PER_P, u=2)
+            for half, copy in enumerate((nc.vector.tensor_copy, nc.scalar.copy)):
+                bank = psum.tile([P, 2, 2, P], F32, tag="turned", name="x_turned")
+                for jj in range(2):
+                    for u in range(2):
+                        nc.tensor.transpose(bank[:, jj, u, :], words[:, 2 * half + jj, u : K_PASS // 2 : 2], identity)
+                copy(out=grouped_words[:, 2 * half : 2 * half + 2, :, :], in_=bank[:].rearrange("p j u r -> p j r u"))
+            x_grouped[g] = grouped
+
+        def quantize_x(g):
+            nc.vector.quantize_mx(
+                out=x_codes[:, g, :].bitcast(E5M2X4), scales=x_scales[:, g, :], in_=x_grouped[g][:]
+            )
+
+        bias_cols = const.tile([P, P], F32)
+        v_bias = const.tile([P, NKV, DH], F32)
+
+        def bias_to_columns():
+            bank = psum.tile([P, TOK_PER_P, P], F32, tag="acc", name="bias_turned")
+            nc.tensor.transpose(bank[:, 0, :], bias_rows32[:], identity)
+            nc.scalar.copy(out=bias_cols[:], in_=bank[:, 0, :])
+
+        def spread_v_bias():
+            bank = psum.tile([P, NKV, DH], F32, tag="acc", name="v_bias_turned")
+            for h in range(NKV):
+                col = NH + NKV + h
+                nc.tensor.transpose(bank[:, h, :], bias_cols[:, col : col + 1].to_broadcast([P, P]), identity)
+            nc.scalar.copy(out=v_bias[:], in_=bank[:])
+
+        transpose_x(0)
+        bias_to_columns()
+        transpose_x(1)
+        quantize_x(0)
+        spread_v_bias()
+        transpose_x(2)
+        quantize_x(1)
+        transpose_x(3)
+        quantize_x(2)
+        quantize_x(3)
+
+        w_grouped = {}
+        w_codes = {}
+        w_scales = {}
+
+        def interleave(copy, n, first, last):
+            if n not in w_grouped:
+                w_grouped[n] = work.tile(
+                    [P, PASSES, PAIR * PACK], BF16, tag="w_grouped", name="w_grouped", align_bytes=64
+                )
+            for g in range(PASSES):
+                lo, hi = max(first - g * PAIR, 0), min(last - g * PAIR, PAIR)
+                if lo >= hi:
+                    continue
+                base = (n % 2) * PAIR
+                src = w_raw[(n // 2, g)][:, :, base + lo : base + hi]
+                dst = w_grouped[n][:, g, lo * PACK : hi * PACK]
+                copy(
+                    out=dst.rearrange("p (c i t) -> p c t i", i=RUN, t=PACK),
+                    in_=src.rearrange("p t (c i) -> p c t i", i=RUN),
+                )
+
+        def quantize_w(n, half):
+            if n not in w_codes:
+                w_codes[n] = work.tile([P, PASSES, PAIR], U32, tag="w_codes", name="w_codes", align_bytes=64)
+                w_scales[n] = work.tile([P, PASSES, PAIR], U8, tag="w_scales", name="w_scales", align_bytes=64)
+            gs = slice(2 * half, 2 * half + 2)
+            nc.vector.quantize_mx(
+                out=w_codes[n][:, gs, :].rearrange("p g c -> p (g c)").bitcast(E4M3X4),
+                scales=w_scales[n][:, gs, :].rearrange("p g c -> p (g c)"),
+                in_=w_grouped[n][:, gs, :].rearrange("p g c -> p (g c)"),
+            )
+
+        acc = {}
+        products = {}
+        turned = {}
+
+        def multiply(n):
+            rotated = pairs[n][5]
+            acc[n] = [psum.tile([P, S], F32, tag="acc", name="acc") for hh in range(2)]
+            if rotated:
+                for g in range(PASSES):
+                    for hh in range(2):
+                        cols = slice(hh * DH, (hh + 1) * DH)
+                        nc.tensor.matmul_mx(
+                            out=acc[n][hh][:],
+                            lhsT=w_codes[n][:, g, cols].bitcast(E4M3X4), lhsT_scale=w_scales[n][:, g, cols],
+                            rhs=x_codes[:, g, :].bitcast(E5M2X4), rhs_scale=x_scales[:, g, :],
+                            start=(g == 0), stop=(g == PASSES - 1),
+                        )
+            else:
+                for hh in range(2):
+                    cols = slice(hh * DH, (hh + 1) * DH)
+                    for j in range(TOK_PER_P):
+                        toks = slice(j * P, (j + 1) * P)
+                        for g in range(PASSES):
+                            nc.tensor.matmul_mx(
+                                out=acc[n][hh][:, j * DH : (j + 1) * DH],
+                                lhsT=x_codes[:, g, toks].bitcast(E5M2X4), lhsT_scale=x_scales[:, g, toks],
+                                rhs=w_codes[n][:, g, cols].bitcast(E4M3X4), rhs_scale=w_scales[n][:, g, cols],
+                                start=(g == 0), stop=(g == PASSES - 1),
+                            )
+
+        def store(n, hh, result):
+            out, head = pairs[n][2], pairs[n][3] + hh
+            nc.sync.dma_start(out=out[0, head].rearrange("(p j) d -> p j d", j=TOK_PER_P), in_=result[:])
+
+        def read_sums(n):
+            for hh in range(2):
+                if pairs[n][5]:
+                    col = pairs[n][4] + hh
+                    both = work.tile([P, 2, S], F32, tag="products", name="products", bufs=4)
+                    for i in range(2):
+                        nc.vector.scalar_tensor_tensor(
+                            out=both[:, i, :], in0=acc[n][hh][:], scalar=bias_cols[:, col : col + 1],
+                            in1=table[:, i, :], op0=ALU.add, op1=ALU.mult,
+                        )
+                    products[(n, hh)] = both
+                else:
+                    head = pairs[n][3] + hh
+                    result = results.tile([P, TOK_PER_P, DH], F32, tag="result", name="result")
+                    nc.vector.tensor_tensor(
+                        out=result[:], in0=acc[n][hh][:].rearrange("p (j d) -> p j d", d=DH),
+                        in1=v_bias[:, head, :].unsqueeze(1).to_broadcast([P, TOK_PER_P, DH]), op=ALU.add,
+                    )
+                    store(n, hh, result)
+
+        def rotate(n):
+            for hh in range(2):
+                bank = psum.tile([P, TOK_PER_P, DH], F32, tag="turned", name="rotated")
+                for j in range(TOK_PER_P):
+                    toks = slice(j * P, (j + 1) * P)
+                    for i, order in enumerate((identity, swap_halves)):
+                        nc.tensor.matmul(
+                            out=bank[:, j, :], lhsT=products[(n, hh)][:, i, toks], rhs=order,
+                            is_transpose=True, start=(i == 0), stop=(i == 1),
+                        )
+                turned[(n, hh)] = bank
+
+        def copy_out(n):
+            for hh in range(2):
+                result = results.tile([P, TOK_PER_P, DH], F32, tag="result", name="result")
+                nc.scalar.copy(out=result[:], in_=turned[(n, hh)][:])
+                store(n, hh, result)
+
+        for half in range(2):
+            first, last = 2 * half * PAIR, 2 * (half + 1) * PAIR
+            interleave(nc.vector.tensor_copy, 0, first, last)
+            interleave(nc.scalar.copy, 1, first, last)
+            quantize_w(0, half)
+            quantize_w(1, half)
+
+        def is_rotated(n):
+            return 0 <= n < n_pairs and pairs[n][5]
+
+        for s in range(n_pairs + 1):
+            if s < n_pairs:
+                multiply(s)
+            if is_rotated(s - 2):
+                copy_out(s - 2)
+            if is_rotated(s - 1):
+                rotate(s - 1)
+            if s + 2 < n_pairs:
+                interleave(nc.vector.tensor_copy, s + 2, 0, VECTOR_COLS)
+                interleave(nc.scalar.copy, s + 2, VECTOR_COLS, PASSES * PAIR)
+            if 2 <= s + 1 < n_pairs:
+                quantize_w(s + 1, 0)
+                quantize_w(s + 1, 1)
+            if s < n_pairs:
+                read_sums(s)

@@ -2,7 +2,6 @@ import math
 from contextlib import ExitStack
 
 import concourse.mybir as mybir
-from concourse.masks import make_identity
 
 S, H, NH, NKV, DH = 512, 2048, 16, 4, 128
 ROPE_THETA = 10000.0
@@ -25,8 +24,15 @@ PASSES = H // K_PASS
 TOK_PER_P = S // P
 CHUNK = 512
 PAIR = 2 * DH
+HEADS = NH + 2 * NKV
 RUN = 4
-VECTOR_COLS = 288
+VECTOR_COLS = 160
+VECTOR_COLS_FIRST = 288
+VECTOR_COLS_START = 0
+ORDER = (("x", 0), ("w", 0), ("x", 1), ("w", 1), ("x", 2), ("w", 2), ("x", 3), ("w", 3))
+XC = 2
+LAG = 1
+LOAD_GROUPS = ((2, 1), (3, 1), (4, 2), (6, 2), (8, 2), (10, 2))
 
 
 def tile_autoreggqaattention_pa_kernel(
@@ -53,18 +59,32 @@ def tile_autoreggqaattention_pa_kernel(
 
         x_rows = hidden_states[0].rearrange("(p j) k -> p j k", j=TOK_PER_P)
         x_raw = []
-        for g in range(PASSES):
+        w_raw = {}
+        bias_rows = const.tile([P, DH], BF16)
+
+        def load_w(n, count, g):
+            w, col0 = pairs[n][0], pairs[n][1]
+            raw = loads.tile([P, PACK, count * PAIR], BF16, tag="raw", name="w_raw")
+            rows = w[g * K_PASS : (g + 1) * K_PASS, col0 : col0 + count * PAIR]
+            nc.sync.dma_start(out=raw[:], in_=rows.rearrange("(p t) c -> p t c", t=PACK))
+            for m in range(count):
+                w_raw[(n + m, g)] = raw[:, :, m * PAIR : (m + 1) * PAIR]
+
+        for vec, row0, heads in ((bq, 0, NH), (bk, NH, NKV), (bv, NH + NKV, NKV)):
+            nc.scalar.dma_start(out=bias_rows[row0 : row0 + heads, :], in_=vec.rearrange("(h d) -> h d", d=DH))
+        def load_x(g):
             raw = loads.tile([P, TOK_PER_P, K_PASS], BF16, tag="raw", name="x_raw")
             nc.sync.dma_start(out=raw[:], in_=x_rows[:, :, g * K_PASS : (g + 1) * K_PASS])
             x_raw.append(raw)
-        w_raw = {}
-        for n in range(0, n_pairs, 2):
-            w, col0 = pairs[n][0], pairs[n][1]
+
+        for kind, g in ORDER:
+            if kind == "x":
+                load_x(g)
+            else:
+                load_w(0, 2, g)
+        for n, count in LOAD_GROUPS:
             for g in range(PASSES):
-                raw = loads.tile([P, PACK, CHUNK], BF16, tag="raw", name="w_raw")
-                rows = w[g * K_PASS : (g + 1) * K_PASS, col0 : col0 + CHUNK]
-                nc.sync.dma_start(out=raw[:], in_=rows.rearrange("(p t) c -> p t c", t=PACK))
-                w_raw[(n // 2, g)] = raw
+                load_w(n, count, g)
 
         channel = const.tile([P, 7], I32)
         nc.gpsimd.iota(channel[:], pattern=[[0, 7]], base=0, channel_multiplier=1)
@@ -75,19 +95,18 @@ def tile_autoreggqaattention_pa_kernel(
             position[:], pattern=[[1, TOK_PER_P], [TOK_PER_P, P]], base=0, channel_multiplier=0,
             allow_small_or_imprecise_dtypes=True,
         )
-        eye = const.tile([P, P + DH // 2], F32)
-        make_identity(nc, eye[:, 0:P])
-        nc.gpsimd.tensor_copy(out=eye[:, P : P + DH // 2], in_=eye[:, 0 : DH // 2])
+        eye = const.tile([P, 2 * P], F32)
+        nc.gpsimd.memset(eye[:], 0.0)
+        nc.gpsimd.affine_select(
+            out=eye[:], in_=eye[:], pattern=[[0, 2], [-1, P]], compare_op=ALU.not_equal, fill=1.0,
+            base=0, channel_multiplier=1,
+        )
         identity = eye[:, 0:P]
         swap_halves = eye[:, DH // 2 : DH // 2 + P]
 
-        bias_rows = const.tile([P, DH], BF16)
-        nc.vector.memset(bias_rows[:], 0.0)
-        nc.scalar.dma_start(out=bias_rows[0:NH, :], in_=bq.rearrange("(h d) -> h d", d=DH))
-        nc.scalar.dma_start(out=bias_rows[NH : NH + NKV, :], in_=bk.rearrange("(h d) -> h d", d=DH))
-        nc.scalar.dma_start(
-            out=bias_rows[NH + NKV : NH + 2 * NKV, :], in_=bv.rearrange("(h d) -> h d", d=DH)
-        )
+        bias_rows32 = const.tile([P, DH], F32)
+        nc.gpsimd.memset(bias_rows32[:], 0.0)
+        nc.gpsimd.tensor_copy(out=bias_rows32[0:HEADS, :], in_=bias_rows[0:HEADS, :])
 
         shifted = const.tile([P, 7], I32)
         nc.vector.tensor_tensor(out=shifted[:], in0=channel[:], in1=shifts[:], op=ALU.logical_shift_right)
@@ -121,8 +140,6 @@ def tile_autoreggqaattention_pa_kernel(
                 out=table[:, i, :], in_=frac[:, i, :], func=ACT.Sin,
                 scale=2.0 * math.pi, bias=2.0 * math.pi * shift_turns[i],
             )
-        bias_rows32 = const.tile([P, DH], F32)
-        nc.vector.tensor_copy(out=bias_rows32[:], in_=bias_rows[:])
 
         x_codes = const.tile([P, PASSES, S], U32, align_bytes=64)
         x_scales = const.tile([P, PASSES, S], U8, align_bytes=64)
@@ -132,7 +149,7 @@ def tile_autoreggqaattention_pa_kernel(
             grouped = work.tile([P, S * PACK], BF16, tag="x_grouped", name="x_grouped", align_bytes=64)
             words = x_raw[g][:].bitcast(F32)
             grouped_words = grouped[:].bitcast(F32).rearrange("p (j r u) -> p j r u", j=TOK_PER_P, u=2)
-            for half, copy in enumerate((nc.vector.tensor_copy, nc.scalar.copy)):
+            for half, copy in enumerate((nc.vector.tensor_copy, nc.vector.tensor_copy if XC == 2 or (XC == 3 and g < 3) else nc.scalar.copy)):
                 bank = psum.tile([P, 2, 2, P], F32, tag="turned", name="x_turned")
                 for jj in range(2):
                     for u in range(2):
@@ -145,31 +162,15 @@ def tile_autoreggqaattention_pa_kernel(
                 out=x_codes[:, g, :].bitcast(E5M2X4), scales=x_scales[:, g, :], in_=x_grouped[g][:]
             )
 
-        bias_cols = const.tile([P, P], F32)
+        bias_cols = const.tile([P, HEADS], F32)
         v_bias = const.tile([P, NKV, DH], F32)
 
-        def bias_to_columns():
-            bank = psum.tile([P, TOK_PER_P, P], F32, tag="acc", name="bias_turned")
-            nc.tensor.transpose(bank[:, 0, :], bias_rows32[:], identity)
-            nc.scalar.copy(out=bias_cols[:], in_=bank[:, 0, :])
-
-        def spread_v_bias():
-            bank = psum.tile([P, NKV, DH], F32, tag="acc", name="v_bias_turned")
+        def turn_v_bias():
+            bank = psum.tile([P, NKV, DH], F32, tag="turned", name="v_bias_turned")
             for h in range(NKV):
                 col = NH + NKV + h
                 nc.tensor.transpose(bank[:, h, :], bias_cols[:, col : col + 1].to_broadcast([P, P]), identity)
-            nc.scalar.copy(out=v_bias[:], in_=bank[:])
-
-        transpose_x(0)
-        bias_to_columns()
-        transpose_x(1)
-        quantize_x(0)
-        spread_v_bias()
-        transpose_x(2)
-        quantize_x(1)
-        transpose_x(3)
-        quantize_x(2)
-        quantize_x(3)
+            return bank
 
         w_grouped = {}
         w_codes = {}
@@ -184,18 +185,18 @@ def tile_autoreggqaattention_pa_kernel(
                 lo, hi = max(first - g * PAIR, 0), min(last - g * PAIR, PAIR)
                 if lo >= hi:
                     continue
-                base = (n % 2) * PAIR
-                src = w_raw[(n // 2, g)][:, :, base + lo : base + hi]
+                src = w_raw[(n, g)][:, :, lo:hi]
                 dst = w_grouped[n][:, g, lo * PACK : hi * PACK]
                 copy(
                     out=dst.rearrange("p (c i t) -> p c t i", i=RUN, t=PACK),
                     in_=src.rearrange("p t (c i) -> p c t i", i=RUN),
                 )
 
+        def new_codes(n):
+            w_codes[n] = work.tile([P, PASSES, PAIR], U32, tag="w_codes", name="w_codes", align_bytes=64)
+            w_scales[n] = work.tile([P, PASSES, PAIR], U8, tag="w_scales", name="w_scales", align_bytes=64)
+
         def quantize_w(n, half):
-            if n not in w_codes:
-                w_codes[n] = work.tile([P, PASSES, PAIR], U32, tag="w_codes", name="w_codes", align_bytes=64)
-                w_scales[n] = work.tile([P, PASSES, PAIR], U8, tag="w_scales", name="w_scales", align_bytes=64)
             gs = slice(2 * half, 2 * half + 2)
             nc.vector.quantize_mx(
                 out=w_codes[n][:, gs, :].rearrange("p g c -> p (g c)").bitcast(E4M3X4),
@@ -203,23 +204,50 @@ def tile_autoreggqaattention_pa_kernel(
                 in_=w_grouped[n][:, gs, :].rearrange("p g c -> p (g c)"),
             )
 
+        last_pass = {}
+
+        def interleave_last_pass(n):
+            grouped = work.tile([P, PAIR * PACK], BF16, tag="last_pass", name="last_pass", bufs=1, align_bytes=64)
+            src = w_raw[(n, PASSES - 1)]
+            if n == 2:
+                nc.scalar.copy(
+                    out=grouped[:].rearrange("p (c i t) -> p c t i", i=RUN, t=PACK),
+                    in_=src.rearrange("p t (c i) -> p c t i", i=RUN),
+                )
+            else:
+                nc.gpsimd.tensor_scalar(
+                    out=grouped[:].rearrange("p (c t) -> p c t", t=PACK), in0=src.rearrange("p t c -> p c t"),
+                    scalar1=1.0, scalar2=0.0, op0=ALU.mult, op1=ALU.add,
+                )
+            last_pass[n] = grouped
+
+        def quantize_pass(n, g, grouped):
+            nc.vector.quantize_mx(
+                out=w_codes[n][:, g, :].bitcast(E4M3X4), scales=w_scales[n][:, g, :], in_=grouped
+            )
+
         acc = {}
         products = {}
         turned = {}
 
-        def multiply(n):
-            rotated = pairs[n][5]
+        def new_sums(n):
             acc[n] = [psum.tile([P, S], F32, tag="acc", name="acc") for hh in range(2)]
-            if rotated:
+
+        def multiply_pass(n, g):
+            for hh in range(2):
+                cols = slice(hh * DH, (hh + 1) * DH)
+                nc.tensor.matmul_mx(
+                    out=acc[n][hh][:],
+                    lhsT=w_codes[n][:, g, cols].bitcast(E4M3X4), lhsT_scale=w_scales[n][:, g, cols],
+                    rhs=x_codes[:, g, :].bitcast(E5M2X4), rhs_scale=x_scales[:, g, :],
+                    start=(g == 0), stop=(g == PASSES - 1),
+                )
+
+        def multiply(n):
+            new_sums(n)
+            if pairs[n][5]:
                 for g in range(PASSES):
-                    for hh in range(2):
-                        cols = slice(hh * DH, (hh + 1) * DH)
-                        nc.tensor.matmul_mx(
-                            out=acc[n][hh][:],
-                            lhsT=w_codes[n][:, g, cols].bitcast(E4M3X4), lhsT_scale=w_scales[n][:, g, cols],
-                            rhs=x_codes[:, g, :].bitcast(E5M2X4), rhs_scale=x_scales[:, g, :],
-                            start=(g == 0), stop=(g == PASSES - 1),
-                        )
+                    multiply_pass(n, g)
             else:
                 for hh in range(2):
                     cols = slice(hh * DH, (hh + 1) * DH)
@@ -275,28 +303,52 @@ def tile_autoreggqaattention_pa_kernel(
                 nc.scalar.copy(out=result[:], in_=turned[(n, hh)][:])
                 store(n, hh, result)
 
-        for half in range(2):
-            first, last = 2 * half * PAIR, 2 * (half + 1) * PAIR
-            interleave(nc.vector.tensor_copy, 0, first, last)
-            interleave(nc.scalar.copy, 1, first, last)
-            quantize_w(0, half)
-            quantize_w(1, half)
+        for n in range(2):
+            new_codes(n)
+            new_sums(n)
+        for g in range(PASSES):
+            cut = g * PAIR + VECTOR_COLS_START
+            interleave(nc.vector.tensor_copy, 0, g * PAIR, cut)
+            interleave(nc.scalar.copy, 0, cut, (g + 1) * PAIR)
+            interleave(nc.scalar.copy, 1, g * PAIR, (g + 1) * PAIR)
+            transpose_x(g)
+            if g == 2:
+                bias_bank = psum.tile([P, P], F32, tag="turned", name="bias_turned")
+                nc.tensor.transpose(bias_bank[:], bias_rows32[:], identity)
+                nc.vector.tensor_copy(out=bias_cols[:], in_=bias_bank[:, 0:HEADS])
+            if g >= LAG:
+                for n in range(2):
+                    multiply_pass(n, g - LAG)
+            quantize_pass(0, g, w_grouped[0][:, g, :])
+            quantize_x(g)
+            quantize_pass(1, g, w_grouped[1][:, g, :])
+        for g in range(PASSES - LAG, PASSES):
+            for n in range(2):
+                multiply_pass(n, g)
+        v_bias_bank = turn_v_bias()
 
         def is_rotated(n):
             return 0 <= n < n_pairs and pairs[n][5]
 
         for s in range(n_pairs + 1):
-            if s < n_pairs:
+            if 2 <= s < n_pairs:
                 multiply(s)
             if is_rotated(s - 2):
                 copy_out(s - 2)
+            if s == 1:
+                nc.scalar.copy(out=v_bias[:], in_=v_bias_bank[:])
             if is_rotated(s - 1):
                 rotate(s - 1)
             if s + 2 < n_pairs:
-                interleave(nc.vector.tensor_copy, s + 2, 0, VECTOR_COLS)
-                interleave(nc.scalar.copy, s + 2, VECTOR_COLS, PASSES * PAIR)
+                share = VECTOR_COLS_FIRST if s == 0 else VECTOR_COLS
+                interleave(nc.vector.tensor_copy, s + 2, 0, share)
+                interleave(nc.scalar.copy, s + 2, share, (PASSES - 1) * PAIR)
             if 2 <= s + 1 < n_pairs:
+                new_codes(s + 1)
                 quantize_w(s + 1, 0)
-                quantize_w(s + 1, 1)
+                quantize_pass(s + 1, 2, w_grouped[s + 1][:, 2, :])
+                quantize_pass(s + 1, 3, last_pass[s + 1][:])
+            if s + 2 < n_pairs:
+                interleave_last_pass(s + 2)
             if s < n_pairs:
                 read_sums(s)

@@ -26,9 +26,10 @@ CHUNK = 512
 PAIR = 2 * DH
 HEADS = NH + 2 * NKV
 RUN = 4
-VECTOR_COLS = 160
-VECTOR_COLS_FIRST = 288
-VECTOR_COLS_START = 0
+GPSIMD_COLS = 160
+VECTOR_COLS = 224
+FIRST_ON_V = 1
+RUN_HEADS = 2
 ORDER = (("x", 0), ("w", 0), ("x", 1), ("w", 1), ("x", 2), ("w", 2), ("x", 3), ("w", 3))
 XC = 2
 LAG = 1
@@ -176,21 +177,27 @@ def tile_autoreggqaattention_pa_kernel(
         w_codes = {}
         w_scales = {}
 
-        def interleave(copy, n, first, last):
-            if n not in w_grouped:
-                w_grouped[n] = work.tile(
-                    [P, PASSES, PAIR * PACK], BF16, tag="w_grouped", name="w_grouped", align_bytes=64
-                )
-            for g in range(PASSES):
-                lo, hi = max(first - g * PAIR, 0), min(last - g * PAIR, PAIR)
-                if lo >= hi:
-                    continue
-                src = w_raw[(n, g)][:, :, lo:hi]
-                dst = w_grouped[n][:, g, lo * PACK : hi * PACK]
-                copy(
-                    out=dst.rearrange("p (c i t) -> p c t i", i=RUN, t=PACK),
-                    in_=src.rearrange("p t (c i) -> p c t i", i=RUN),
-                )
+        def new_grouped(n, half, tag, bufs):
+            tile = work.tile([P, 2, PAIR * PACK], BF16, tag=tag, name=tag, bufs=bufs, align_bytes=64)
+            w_grouped[(n, half)] = tile
+
+        def interleave(copy, n, g, lo, hi):
+            if lo >= hi:
+                return
+            src = w_raw[(n, g)][:, :, lo:hi]
+            dst = w_grouped[(n, g // 2)][:, g % 2, lo * PACK : hi * PACK]
+            copy(
+                out=dst.rearrange("p (c i t) -> p c t i", i=RUN, t=PACK),
+                in_=src.rearrange("p t (c i) -> p c t i", i=RUN),
+            )
+
+        def interleave_on_gpsimd(n, g, lo, hi):
+            dst = w_grouped[(n, g // 2)][:, g % 2, lo * PACK : hi * PACK]
+            nc.gpsimd.tensor_scalar(
+                out=dst.rearrange("p (c t) -> p c t", t=PACK),
+                in0=w_raw[(n, g)][:, :, lo:hi].rearrange("p t c -> p c t"),
+                scalar1=1.0, scalar2=0.0, op0=ALU.mult, op1=ALU.add,
+            )
 
         def new_codes(n):
             w_codes[n] = work.tile([P, PASSES, PAIR], U32, tag="w_codes", name="w_codes", align_bytes=64)
@@ -201,25 +208,8 @@ def tile_autoreggqaattention_pa_kernel(
             nc.vector.quantize_mx(
                 out=w_codes[n][:, gs, :].rearrange("p g c -> p (g c)").bitcast(E4M3X4),
                 scales=w_scales[n][:, gs, :].rearrange("p g c -> p (g c)"),
-                in_=w_grouped[n][:, gs, :].rearrange("p g c -> p (g c)"),
+                in_=w_grouped[(n, half)][:].rearrange("p g c -> p (g c)"),
             )
-
-        last_pass = {}
-
-        def interleave_last_pass(n):
-            grouped = work.tile([P, PAIR * PACK], BF16, tag="last_pass", name="last_pass", bufs=1, align_bytes=64)
-            src = w_raw[(n, PASSES - 1)]
-            if n == 2:
-                nc.scalar.copy(
-                    out=grouped[:].rearrange("p (c i t) -> p c t i", i=RUN, t=PACK),
-                    in_=src.rearrange("p t (c i) -> p c t i", i=RUN),
-                )
-            else:
-                nc.gpsimd.tensor_scalar(
-                    out=grouped[:].rearrange("p (c t) -> p c t", t=PACK), in0=src.rearrange("p t c -> p c t"),
-                    scalar1=1.0, scalar2=0.0, op0=ALU.mult, op1=ALU.add,
-                )
-            last_pass[n] = grouped
 
         def quantize_pass(n, g, grouped):
             nc.vector.quantize_mx(
@@ -249,41 +239,36 @@ def tile_autoreggqaattention_pa_kernel(
                 for g in range(PASSES):
                     multiply_pass(n, g)
             else:
-                for hh in range(2):
-                    cols = slice(hh * DH, (hh + 1) * DH)
-                    for j in range(TOK_PER_P):
-                        toks = slice(j * P, (j + 1) * P)
-                        for g in range(PASSES):
-                            nc.tensor.matmul_mx(
-                                out=acc[n][hh][:, j * DH : (j + 1) * DH],
-                                lhsT=x_codes[:, g, toks].bitcast(E5M2X4), lhsT_scale=x_scales[:, g, toks],
-                                rhs=w_codes[n][:, g, cols].bitcast(E4M3X4), rhs_scale=w_scales[n][:, g, cols],
-                                start=(g == 0), stop=(g == PASSES - 1),
-                            )
-
-        def store(n, hh, result):
-            out, head = pairs[n][2], pairs[n][3] + hh
-            nc.sync.dma_start(out=out[0, head].rearrange("(p j) d -> p j d", j=TOK_PER_P), in_=result[:])
+                for j in range(TOK_PER_P):
+                    toks = slice(j * P, (j + 1) * P)
+                    for g in range(PASSES):
+                        nc.tensor.matmul_mx(
+                            out=acc[n][j // 2][:, (j % 2) * PAIR : (j % 2 + 1) * PAIR],
+                            lhsT=x_codes[:, g, toks].bitcast(E5M2X4), lhsT_scale=x_scales[:, g, toks],
+                            rhs=w_codes[n][:, g, :].bitcast(E4M3X4), rhs_scale=w_scales[n][:, g, :],
+                            start=(g == 0), stop=(g == PASSES - 1),
+                        )
 
         def read_sums(n):
             for hh in range(2):
                 if pairs[n][5]:
                     col = pairs[n][4] + hh
                     both = work.tile([P, 2, S], F32, tag="products", name="products", bufs=4)
-                    for i in range(2):
-                        nc.vector.scalar_tensor_tensor(
-                            out=both[:, i, :], in0=acc[n][hh][:], scalar=bias_cols[:, col : col + 1],
-                            in1=table[:, i, :], op0=ALU.add, op1=ALU.mult,
-                        )
+                    nc.vector.scalar_tensor_tensor(
+                        out=both[:], in0=acc[n][hh][:].unsqueeze(1).to_broadcast([P, 2, S]),
+                        scalar=bias_cols[:, col : col + 1], in1=table[:], op0=ALU.add, op1=ALU.mult,
+                    )
                     products[(n, hh)] = both
                 else:
-                    head = pairs[n][3] + hh
-                    result = results.tile([P, TOK_PER_P, DH], F32, tag="result", name="result")
+                    out, head = pairs[n][2], pairs[n][3]
+                    result = results.tile([P, 2, 2, DH], F32, tag="result", name="result")
                     nc.vector.tensor_tensor(
-                        out=result[:], in0=acc[n][hh][:].rearrange("p (j d) -> p j d", d=DH),
-                        in1=v_bias[:, head, :].unsqueeze(1).to_broadcast([P, TOK_PER_P, DH]), op=ALU.add,
+                        out=result[:].rearrange("p h j d -> p j h d"),
+                        in0=acc[n][hh][:].rearrange("p (j h d) -> p j h d", j=2, h=2),
+                        in1=v_bias[:, head : head + 2, :].unsqueeze(1).to_broadcast([P, 2, 2, DH]), op=ALU.add,
                     )
-                    store(n, hh, result)
+                    rows = out[0, head : head + 2].rearrange("h (p j) d -> p h j d", j=TOK_PER_P)
+                    nc.sync.dma_start(out=rows[:, :, 2 * hh : 2 * hh + 2, :], in_=result[:])
 
         def rotate(n):
             for hh in range(2):
@@ -301,16 +286,17 @@ def tile_autoreggqaattention_pa_kernel(
             for hh in range(2):
                 result = results.tile([P, TOK_PER_P, DH], F32, tag="result", name="result")
                 nc.scalar.copy(out=result[:], in_=turned[(n, hh)][:])
-                store(n, hh, result)
+                out, head = pairs[n][2], pairs[n][3] + hh
+                nc.sync.dma_start(out=out[0, head].rearrange("(p j) d -> p j d", j=TOK_PER_P), in_=result[:])
 
         for n in range(2):
             new_codes(n)
             new_sums(n)
         for g in range(PASSES):
-            cut = g * PAIR + VECTOR_COLS_START
-            interleave(nc.vector.tensor_copy, 0, g * PAIR, cut)
-            interleave(nc.scalar.copy, 0, cut, (g + 1) * PAIR)
-            interleave(nc.scalar.copy, 1, g * PAIR, (g + 1) * PAIR)
+            for n in range(2):
+                if g % 2 == 0:
+                    new_grouped(n, g // 2, "w_early", 4)
+                interleave(nc.scalar.copy, n, g, 0, PAIR)
             transpose_x(g)
             if g == 2:
                 bias_bank = psum.tile([P, P], F32, tag="turned", name="bias_turned")
@@ -319,9 +305,9 @@ def tile_autoreggqaattention_pa_kernel(
             if g >= LAG:
                 for n in range(2):
                     multiply_pass(n, g - LAG)
-            quantize_pass(0, g, w_grouped[0][:, g, :])
+            quantize_pass(0, g, w_grouped[(0, g // 2)][:, g % 2, :])
             quantize_x(g)
-            quantize_pass(1, g, w_grouped[1][:, g, :])
+            quantize_pass(1, g, w_grouped[(1, g // 2)][:, g % 2, :])
         for g in range(PASSES - LAG, PASSES):
             for n in range(2):
                 multiply_pass(n, g)
@@ -340,15 +326,21 @@ def tile_autoreggqaattention_pa_kernel(
             if is_rotated(s - 1):
                 rotate(s - 1)
             if s + 2 < n_pairs:
-                share = VECTOR_COLS_FIRST if s == 0 else VECTOR_COLS
-                interleave(nc.vector.tensor_copy, s + 2, 0, share)
-                interleave(nc.scalar.copy, s + 2, share, (PASSES - 1) * PAIR)
+                new_grouped(s + 2, 0, "w_early", 4)
+                interleave(nc.scalar.copy, s + 2, 0, 0, PAIR)
+                interleave(nc.scalar.copy, s + 2, 1, 0, PAIR)
             if 2 <= s + 1 < n_pairs:
                 new_codes(s + 1)
+                interleave(nc.vector.tensor_copy, s + 1, 2, 0, VECTOR_COLS)
                 quantize_w(s + 1, 0)
-                quantize_pass(s + 1, 2, w_grouped[s + 1][:, 2, :])
-                quantize_pass(s + 1, 3, last_pass[s + 1][:])
+                quantize_w(s + 1, 1)
             if s + 2 < n_pairs:
-                interleave_last_pass(s + 2)
+                new_grouped(s + 2, 1, "w_late", 1)
+                if s > 0:
+                    interleave_on_gpsimd(s + 2, 3, 0, GPSIMD_COLS)
+                else:
+                    interleave(nc.vector.tensor_copy if FIRST_ON_V else nc.scalar.copy, s + 2, 3, 0, GPSIMD_COLS)
+                interleave(nc.scalar.copy, s + 2, 3, GPSIMD_COLS, PAIR)
+                interleave(nc.scalar.copy, s + 2, 2, VECTOR_COLS, PAIR)
             if s < n_pairs:
                 read_sums(s)

import math
from contextlib import ExitStack

import concourse.mybir as mybir

S, H, NH, NKV, DH = 512, 2048, 16, 4, 128
ROPE_THETA = 10000.0
FLOPS = 2 * S * H * (NH + 2 * NKV) * DH

F32 = mybir.dt.float32
BF16 = mybir.dt.bfloat16
I32 = mybir.dt.int32
U32 = mybir.dt.uint32
U8 = mybir.dt.uint8
E4M3X4 = mybir.dt.float8_e4m3fn_x4
E5M2X4 = mybir.dt.float8_e5m2_x4
ALU = mybir.AluOpType
ACT = mybir.ActivationFunctionType

P = 128
PACK = 4
K_PASS = P * PACK
PASSES = H // K_PASS
TOK_PER_P = S // P
CHUNK = 512
PAIR = 2 * DH
HEADS = NH + 2 * NKV
RUN = 4
GPSIMD_COLS = 160
VECTOR_COLS = 224
FIRST_ON_V = 1
RUN_HEADS = 2
ORDER = (("x", 0), ("w", 0), ("x", 1), ("w", 1), ("x", 2), ("w", 2), ("x", 3), ("w", 3))
XC = 2
LAG = 1
LOAD_GROUPS = ((2, 1), (3, 1), (4, 2), (6, 2), (8, 2), (10, 2))


def tile_autoreggqaattention_pa_kernel(
    tc, hidden_states, Wq, bq, Wk, bk, Wv, bv, out_0, out_1, out_2
):
    nc = tc.nc
    pairs = []
    for w, out, heads, bias0, rotated in (
        (Wk, out_1, NKV, NH, True),
        (Wq, out_0, NH, 0, True),
        (Wv, out_2, NKV, NH + NKV, False),
    ):
        for h in range(0, heads, 2):
            pairs.append((w, h * DH, out, h, bias0 + h, rotated))
    n_pairs = len(pairs)

    with ExitStack() as ctx:
        const = ctx.enter_context(tc.tile_pool(name="const", bufs=1))
        loads = ctx.enter_context(tc.tile_pool(name="loads", bufs=16))
        work = ctx.enter_context(tc.tile_pool(name="work", bufs=3))
        results = ctx.enter_context(tc.tile_pool(name="results", bufs=20))
        psum = ctx.enter_context(tc.psum_pool(name="psum", bufs=4))
        ctx.enter_context(tc.manual_schedule())

        x_rows = hidden_states[0].rearrange("(p j) k -> p j k", j=TOK_PER_P)
        x_raw = []
        w_raw = {}
        bias_rows = const.tile([P, DH], BF16)

        def load_w(n, count, g):
            w, col0 = pairs[n][0], pairs[n][1]
            raw = loads.tile([P, PACK, count * PAIR], BF16, tag="raw", name="w_raw")
            rows = w[g * K_PASS : (g + 1) * K_PASS, col0 : col0 + count * PAIR]
            nc.sync.dma_start(out=raw[:], in_=rows.rearrange("(p t) c -> p t c", t=PACK))
            for m in range(count):
                w_raw[(n + m, g)] = raw[:, :, m * PAIR : (m + 1) * PAIR]

        for vec, row0, heads in ((bq, 0, NH), (bk, NH, NKV), (bv, NH + NKV, NKV)):
            nc.scalar.dma_start(out=bias_rows[row0 : row0 + heads, :], in_=vec.rearrange("(h d) -> h d", d=DH))
        def load_x(g):
            raw = loads.tile([P, TOK_PER_P, K_PASS], BF16, tag="raw", name="x_raw")
            nc.sync.dma_start(out=raw[:], in_=x_rows[:, :, g * K_PASS : (g + 1) * K_PASS])
            x_raw.append(raw)

        for kind, g in ORDER:
            if kind == "x":
                load_x(g)
            else:
                load_w(0, 2, g)
        for n, count in LOAD_GROUPS:
            for g in range(PASSES):
                load_w(n, count, g)

        channel = const.tile([P, 7], I32)
        nc.gpsimd.iota(channel[:], pattern=[[0, 7]], base=0, channel_multiplier=1)
        shifts = const.tile([P, 7], I32)
        nc.gpsimd.iota(shifts[:], pattern=[[1, 7]], base=0, channel_multiplier=0)
        position = const.tile([P, S], F32)
        nc.gpsimd.iota(
            position[:], pattern=[[1, TOK_PER_P], [TOK_PER_P, P]], base=0, channel_multiplier=0,
            allow_small_or_imprecise_dtypes=True,
        )
        eye = const.tile([P, 2 * P], F32)
        nc.gpsimd.memset(eye[:], 0.0)
        nc.gpsimd.affine_select(
            out=eye[:], in_=eye[:], pattern=[[0, 2], [-1, P]], compare_op=ALU.not_equal, fill=1.0,
            base=0, channel_multiplier=1,
        )
        identity = eye[:, 0:P]
        swap_halves = eye[:, DH // 2 : DH // 2 + P]

        bias_rows32 = const.tile([P, DH], F32)
        nc.gpsimd.memset(bias_rows32[:], 0.0)
        nc.gpsimd.tensor_copy(out=bias_rows32[0:HEADS, :], in_=bias_rows[0:HEADS, :])

        shifted = const.tile([P, 7], I32)
        nc.vector.tensor_tensor(out=shifted[:], in0=channel[:], in1=shifts[:], op=ALU.logical_shift_right)
        bits = const.tile([P, 7], I32)
        nc.vector.tensor_scalar(out=bits[:], in0=shifted[:], scalar1=1, scalar2=None, op0=ALU.bitwise_and)
        factors = const.tile([P, 7], F32)
        turn = 1.0 / (2.0 * math.pi)
        for b in range(7):
            off, on = (1.0, ROPE_THETA ** (-(2**b) / 64)) if b < 6 else (turn, -turn)
            nc.vector.tensor_scalar(
                out=factors[:, b : b + 1], in0=bits[:, b : b + 1], scalar1=on - off, scalar2=off,
                op0=ALU.mult, op1=ALU.add,
            )
        freq = const.tile([P, 1], F32)
        nc.vector.tensor_reduce(out=freq[:], in_=factors[:], axis=mybir.AxisListType.X, op=ALU.mult)
        whole = const.tile([P, 2, S], I32)
        frac = const.tile([P, 2, S], F32)
        table = const.tile([P, 2, S], F32)
        shift_turns = (0.25, 0.0)
        for i in range(2):
            nc.vector.tensor_scalar(
                out=whole[:, i, :], in0=position[:], scalar1=freq[:], scalar2=shift_turns[i],
                op0=ALU.mult, op1=ALU.add,
            )
        for i in range(2):
            nc.vector.scalar_tensor_tensor(
                out=frac[:, i, :], in0=position[:], scalar=freq[:], in1=whole[:, i, :],
                op0=ALU.mult, op1=ALU.subtract,
            )
            nc.scalar.activation(
                out=table[:, i, :], in_=frac[:, i, :], func=ACT.Sin,
                scale=2.0 * math.pi, bias=2.0 * math.pi * shift_turns[i],
            )

        x_codes = const.tile([P, PASSES, S], U32, align_bytes=64)
        x_scales = const.tile([P, PASSES, S], U8, align_bytes=64)
        x_grouped = {}

        def transpose_x(g):
            grouped = work.tile([P, S * PACK], BF16, tag="x_grouped", name="x_grouped", align_bytes=64)
            words = x_raw[g][:].bitcast(F32)
            grouped_words = grouped[:].bitcast(F32).rearrange("p (j r u) -> p j r u", j=TOK_PER_P, u=2)
            for half, copy in enumerate((nc.vector.tensor_copy, nc.vector.tensor_copy if XC == 2 or (XC == 3 and g < 3) else nc.scalar.copy)):
                bank = psum.tile([P, 2, 2, P], F32, tag="turned", name="x_turned")
                for jj in range(2):
                    for u in range(2):
                        nc.tensor.transpose(bank[:, jj, u, :], words[:, 2 * half + jj, u : K_PASS // 2 : 2], identity)
                copy(out=grouped_words[:, 2 * half : 2 * half + 2, :, :], in_=bank[:].rearrange("p j u r -> p j r u"))
            x_grouped[g] = grouped

        def quantize_x(g):
            nc.vector.quantize_mx(
                out=x_codes[:, g, :].bitcast(E5M2X4), scales=x_scales[:, g, :], in_=x_grouped[g][:]
            )

        bias_cols = const.tile([P, HEADS], F32)
        v_bias = const.tile([P, NKV, DH], F32)

        def turn_v_bias():
            bank = psum.tile([P, NKV, DH], F32, tag="turned", name="v_bias_turned")
            for h in range(NKV):
                col = NH + NKV + h
                nc.tensor.transpose(bank[:, h, :], bias_cols[:, col : col + 1].to_broadcast([P, P]), identity)
            return bank

        w_grouped = {}
        w_codes = {}
        w_scales = {}

        def new_grouped(n, half, tag, bufs):
            tile = work.tile([P, 2, PAIR * PACK], BF16, tag=tag, name=tag, bufs=bufs, align_bytes=64)
            w_grouped[(n, half)] = tile

        def interleave(copy, n, g, lo, hi):
            if lo >= hi:
                return
            src = w_raw[(n, g)][:, :, lo:hi]
            dst = w_grouped[(n, g // 2)][:, g % 2, lo * PACK : hi * PACK]
            copy(
                out=dst.rearrange("p (c i t) -> p c t i", i=RUN, t=PACK),
                in_=src.rearrange("p t (c i) -> p c t i", i=RUN),
            )

        def interleave_on_gpsimd(n, g, lo, hi):
            dst = w_grouped[(n, g // 2)][:, g % 2, lo * PACK : hi * PACK]
            nc.gpsimd.tensor_scalar(
                out=dst.rearrange("p (c t) -> p c t", t=PACK),
                in0=w_raw[(n, g)][:, :, lo:hi].rearrange("p t c -> p c t"),
                scalar1=1.0, scalar2=0.0, op0=ALU.mult, op1=ALU.add,
            )

        def new_codes(n):
            w_codes[n] = work.tile([P, PASSES, PAIR], U32, tag="w_codes", name="w_codes", align_bytes=64)
            w_scales[n] = work.tile([P, PASSES, PAIR], U8, tag="w_scales", name="w_scales", align_bytes=64)

        def quantize_w(n, half):
            gs = slice(2 * half, 2 * half + 2)
            nc.vector.quantize_mx(
                out=w_codes[n][:, gs, :].rearrange("p g c -> p (g c)").bitcast(E4M3X4),
                scales=w_scales[n][:, gs, :].rearrange("p g c -> p (g c)"),
                in_=w_grouped[(n, half)][:].rearrange("p g c -> p (g c)"),
            )

        def quantize_pass(n, g, grouped):
            nc.vector.quantize_mx(
                out=w_codes[n][:, g, :].bitcast(E4M3X4), scales=w_scales[n][:, g, :], in_=grouped
            )

        acc = {}
        products = {}
        turned = {}

        def new_sums(n):
            acc[n] = [psum.tile([P, S], F32, tag="acc", name="acc") for hh in range(2)]

        def multiply_pass(n, g):
            for hh in range(2):
                cols = slice(hh * DH, (hh + 1) * DH)
                nc.tensor.matmul_mx(
                    out=acc[n][hh][:],
                    lhsT=w_codes[n][:, g, cols].bitcast(E4M3X4), lhsT_scale=w_scales[n][:, g, cols],
                    rhs=x_codes[:, g, :].bitcast(E5M2X4), rhs_scale=x_scales[:, g, :],
                    start=(g == 0), stop=(g == PASSES - 1),
                )

        def multiply(n):
            new_sums(n)
            if pairs[n][5]:
                for g in range(PASSES):
                    multiply_pass(n, g)
            else:
                for j in range(TOK_PER_P):
                    toks = slice(j * P, (j + 1) * P)
                    for g in range(PASSES):
                        nc.tensor.matmul_mx(
                            out=acc[n][j // 2][:, (j % 2) * PAIR : (j % 2 + 1) * PAIR],
                            lhsT=x_codes[:, g, toks].bitcast(E5M2X4), lhsT_scale=x_scales[:, g, toks],
                            rhs=w_codes[n][:, g, :].bitcast(E4M3X4), rhs_scale=w_scales[n][:, g, :],
                            start=(g == 0), stop=(g == PASSES - 1),
                        )

        def read_sums(n):
            for hh in range(2):
                if pairs[n][5]:
                    col = pairs[n][4] + hh
                    both = work.tile([P, 2, S], F32, tag="products", name="products", bufs=4)
                    nc.vector.scalar_tensor_tensor(
                        out=both[:], in0=acc[n][hh][:].unsqueeze(1).to_broadcast([P, 2, S]),
                        scalar=bias_cols[:, col : col + 1], in1=table[:], op0=ALU.add, op1=ALU.mult,
                    )
                    products[(n, hh)] = both
                else:
                    out, head = pairs[n][2], pairs[n][3]
                    result = results.tile([P, 2, 2, DH], F32, tag="result", name="result")
                    nc.vector.tensor_tensor(
                        out=result[:].rearrange("p h j d -> p j h d"),
                        in0=acc[n][hh][:].rearrange("p (j h d) -> p j h d", j=2, h=2),
                        in1=v_bias[:, head : head + 2, :].unsqueeze(1).to_broadcast([P, 2, 2, DH]), op=ALU.add,
                    )
                    rows = out[0, head : head + 2].rearrange("h (p j) d -> p h j d", j=TOK_PER_P)
                    nc.sync.dma_start(out=rows[:, :, 2 * hh : 2 * hh + 2, :], in_=result[:])

        def rotate(n):
            for hh in range(2):
                bank = psum.tile([P, TOK_PER_P, DH], F32, tag="turned", name="rotated")
                for j in range(TOK_PER_P):
                    toks = slice(j * P, (j + 1) * P)
                    for i, order in enumerate((identity, swap_halves)):
                        nc.tensor.matmul(
                            out=bank[:, j, :], lhsT=products[(n, hh)][:, i, toks], rhs=order,
                            is_transpose=True, start=(i == 0), stop=(i == 1),
                        )
                turned[(n, hh)] = bank

        def copy_out(n):
            for hh in range(2):
                result = results.tile([P, TOK_PER_P, DH], F32, tag="result", name="result")
                nc.scalar.copy(out=result[:], in_=turned[(n, hh)][:])
                out, head = pairs[n][2], pairs[n][3] + hh
                nc.sync.dma_start(out=out[0, head].rearrange("(p j) d -> p j d", j=TOK_PER_P), in_=result[:])

        for n in range(2):
            new_codes(n)
            new_sums(n)
        for g in range(PASSES):
            for n in range(2):
                if g % 2 == 0:
                    new_grouped(n, g // 2, "w_early", 4)
                interleave(nc.scalar.copy, n, g, 0, PAIR)
            transpose_x(g)
            if g == 2:
                bias_bank = psum.tile([P, P], F32, tag="turned", name="bias_turned")
                nc.tensor.transpose(bias_bank[:], bias_rows32[:], identity)
                nc.vector.tensor_copy(out=bias_cols[:], in_=bias_bank[:, 0:HEADS])
            if g >= LAG:
                for n in range(2):
                    multiply_pass(n, g - LAG)
            quantize_pass(0, g, w_grouped[(0, g // 2)][:, g % 2, :])
            quantize_x(g)
            quantize_pass(1, g, w_grouped[(1, g // 2)][:, g % 2, :])
        for g in range(PASSES - LAG, PASSES):
            for n in range(2):
                multiply_pass(n, g)
        v_bias_bank = turn_v_bias()

        def is_rotated(n):
            return 0 <= n < n_pairs and pairs[n][5]

        for s in range(n_pairs + 1):
            if 2 <= s < n_pairs:
                multiply(s)
            if is_rotated(s - 2):
                copy_out(s - 2)
            if s == 1:
                nc.scalar.copy(out=v_bias[:], in_=v_bias_bank[:])
            if is_rotated(s - 1):
                rotate(s - 1)
            if s + 2 < n_pairs:
                new_grouped(s + 2, 0, "w_early", 4)
                interleave(nc.scalar.copy, s + 2, 0, 0, PAIR)
                interleave(nc.scalar.copy, s + 2, 1, 0, PAIR)
            if 2 <= s + 1 < n_pairs:
                new_codes(s + 1)
                interleave(nc.vector.tensor_copy, s + 1, 2, 0, VECTOR_COLS)
                quantize_w(s + 1, 0)
                quantize_w(s + 1, 1)
            if s + 2 < n_pairs:
                new_grouped(s + 2, 1, "w_late", 1)
                if s > 0:
                    interleave_on_gpsimd(s + 2, 3, 0, GPSIMD_COLS)
                else:
                    interleave(nc.vector.tensor_copy if FIRST_ON_V else nc.scalar.copy, s + 2, 3, 0, GPSIMD_COLS)
                interleave(nc.scalar.copy, s + 2, 3, GPSIMD_COLS, PAIR)
                interleave(nc.scalar.copy, s + 2, 2, VECTOR_COLS, PAIR)
            if s < n_pairs:
                read_sums(s)
